import numpy as np
import ml_dtypes


def mxq(x, axis, fmt="e4m3"):
    dtype, down = {"e4m3": (ml_dtypes.float8_e4m3fn, 7), "e5m2": (ml_dtypes.float8_e5m2, 14)}[fmt]
    v = np.moveaxis(np.asarray(x, np.float32).astype(ml_dtypes.bfloat16).astype(np.float64), axis, -1)
    blocks = v.reshape(v.shape[:-1] + (-1, 32))
    amax = np.abs(blocks).max(-1, keepdims=True)
    byte = np.maximum(np.where(amax > 0, np.frexp(amax)[1] - 1 + 127, 0) - down, 1)
    scale = np.exp2(byte - 127.0)
    codes = (blocks / scale).astype(np.float32).astype(dtype).astype(np.float64)
    return np.moveaxis((codes * scale).reshape(v.shape), -1, axis)


WIDE = False


def mx_kscale(k):
    if not WIDE:
        return np.ones(k)
    levels = np.array([10, -10, 5, -5, 0])
    a = np.random.permutation(np.resize(levels, k // 512 * 4)).reshape(k // 512, 4)
    idx = np.arange(k)
    return np.exp2(a[idx // 512, idx % 128 // 32])


BF16 = ml_dtypes.bfloat16


def bf(x):
    return np.asarray(x, np.float32).astype(BF16)


def f64(x):
    return np.asarray(x).astype(np.float64)


B, CI, CO, N, KM, M = 2, 128, 128, 1024, 32, 512
R = 6.0
A = np.sqrt(R) / N ** 0.25


def setup_inputs():
    u = mx_kscale(CI * KM)[::KM]
    t = mx_kscale(M)
    return {
        "x": bf((np.random.standard_normal((B, CI, N)) + A) * u[None, :, None]),
        "wbases": bf((np.random.standard_normal((B, N, M)) + A) / (R * np.sqrt(N))),
        "bases": bf(np.random.standard_normal((B, N, M)) / np.sqrt(M) / t),
        "weights": bf(np.random.standard_normal((CI, CO, KM)) / np.sqrt(CI * KM) / u[:, None, None]),
        "D": bf(np.random.standard_normal((KM, M)) * t),
    }


def reference(x, wbases, bases, weights, D):
    x_hat = f64(x) @ f64(wbases)[:, :, :M]
    z = (x_hat[:, :, None, :] * f64(D)[None, None, :, :]).reshape(B, CI * KM, M)
    w2 = f64(weights).transpose(0, 2, 1).reshape(CI * KM, CO)
    y_hat = mxq(w2, 0, "e4m3").T @ mxq(z, 1, "e4m3")
    return mxq(y_hat, 2, "e4m3") @ mxq(f64(bases)[:, :, :M], 2, "e4m3").transpose(0, 2, 1)

@@ -1,0 +1,201 @@
+from contextlib import ExitStack
+
+import concourse.mybir as mybir
+from concourse.masks import make_identity
+
+F32 = mybir.dt.float32
+BF16 = mybir.dt.bfloat16
+U32 = mybir.dt.uint32
+U8 = mybir.dt.uint8
+FP8X4 = mybir.dt.float8_e4m3fn_x4
+MULT = mybir.AluOpType.mult
+
+NB, CI, CO, NPTS, KM, NM = 2, 128, 128, 1024, 32, 512
+P = 128
+NG = NPTS // P
+NKC = NM // P
+NC = CI * KM // 512
+FLOPS = 2 * NB * (CI * NPTS * NM + CI * KM * CO * NM + CO * NM * NPTS)
+
+
+def tile_phydgalerkinconv_kernel(tc, x, wbases, bases, weights, D, out):
+    nc = tc.nc
+    with ExitStack() as ctx:
+        keep = ctx.enter_context(tc.tile_pool(name="keep", bufs=1))
+        work = ctx.enter_context(tc.tile_pool(name="work", bufs=3))
+        psum = ctx.enter_context(tc.psum_pool(name="psum", bufs=2))
+
+        ident_b = keep.tile([P, P], BF16, name="ident_b")
+        make_identity(nc, ident_b[:])
+        ident_f = keep.tile([P, P], F32, name="ident_f")
+        make_identity(nc, ident_f[:])
+
+        x_sb = [keep.tile([P, NPTS], BF16, name="x_sb%d" % b) for b in range(NB)]
+        wb_sb = [keep.tile([P, NG, NM], BF16, name="wb_sb%d" % b) for b in range(NB)]
+        bs_sb = [keep.tile([P, NG, NM], BF16, name="bs_sb%d" % b) for b in range(NB)]
+        d_load = keep.tile([P, 4 * NM], BF16, name="d_load")
+        w_om = keep.tile([P, CI * KM], BF16, name="w_om")
+
+        nc.sync.dma_start(out=x_sb[0][:], in_=x[0])
+        wb0 = wbases[0].rearrange("(g p) k -> p g k", p=P)
+        for kc in range(NKC):
+            nc.sync.dma_start(out=wb_sb[0][:, :, kc * P:(kc + 1) * P], in_=wb0[:, :, kc * P:(kc + 1) * P])
+        for r in range(8):
+            nc.scalar.dma_start(
+                out=d_load[r:P:8, :],
+                in_=D[4 * r:4 * r + 4, :].rearrange("t k -> (t k)").partition_broadcast(16),
+            )
+        for q in range(4):
+            nc.sync.dma_start(
+                out=w_om[:, 1024 * q:1024 * (q + 1)].rearrange("o (i j) -> o i j", j=KM),
+                in_=weights[32 * q:32 * (q + 1)].rearrange("i o j -> o i j"),
+            )
+        nc.sync.dma_start(out=x_sb[1][:], in_=x[1])
+        nc.sync.dma_start(out=wb_sb[1][:], in_=wbases[1].rearrange("(g p) k -> p g k", p=P))
+        for b in range(NB):
+            nc.sync.dma_start(out=bs_sb[b][:], in_=bases[b].rearrange("(g p) k -> p g k", p=P))
+
+        d_rep = keep.tile([P, NM, 4], BF16, name="d_rep")
+        nc.vector.tensor_copy(out=d_rep[:], in_=d_load[:].rearrange("p (t k) -> p k t", t=4))
+
+        x_t = [keep.tile([P, NG, CI], BF16, name="x_t%d" % b) for b in range(NB)]
+
+        def transpose_x(b, engine):
+            xt_ps = psum.tile([P, NG, CI], BF16, tag="aux", name="xt_ps")
+            for g in range(NG):
+                nc.tensor.transpose(xt_ps[:, g, :], x_sb[b][:, g * P:(g + 1) * P], ident_b[:])
+            if engine == "v":
+                nc.vector.tensor_copy(out=x_t[b][:], in_=xt_ps[:])
+            else:
+                nc.scalar.copy(out=x_t[b][:], in_=xt_ps[:])
+
+        w_grp = keep.tile([P, NC * CO * 4], BF16, name="w_grp", align_bytes=64)
+        w_code = keep.tile([P, NC * CO], U32, name="w_code", align_bytes=64)
+        w_scale = keep.tile([P, NC * CO], U8, name="w_scale", align_bytes=64)
+
+        def prepare_weights():
+            words = w_om[:].bitcast(F32).rearrange("o (c p u) -> o c p u", c=NC, u=2)
+            grp_words = w_grp[:].bitcast(F32).rearrange("p (c o u) -> p c o u", c=NC, u=2)
+            for cp in range(NC // 2):
+                wt_ps = psum.tile([P, 2, 2, CO], F32, tag="aux", name="wt_ps")
+                for cc in range(2):
+                    for u in range(2):
+                        nc.tensor.transpose(wt_ps[:, cc, u, :], words[:, 2 * cp + cc, :, u], ident_f[:])
+                nc.scalar.copy(
+                    out=grp_words[:, 2 * cp:2 * cp + 2, :, :],
+                    in_=wt_ps[:].rearrange("p c u o -> p c o u"),
+                )
+            nc.vector.quantize_mx(out=w_code[:].bitcast(FP8X4), scales=w_scale[:], in_=w_grp[:])
+
+        b_grp = [keep.tile([P, NPTS * 4], BF16, name="b_grp%d" % b, align_bytes=64) for b in range(NB)]
+        b_code = [keep.tile([P, NPTS], U32, name="b_code%d" % b, align_bytes=64) for b in range(NB)]
+        b_scale = [keep.tile([P, NPTS], U8, name="b_scale%d" % b, align_bytes=64) for b in range(NB)]
+
+        def transpose_bases(b, gp):
+            bt_ps = psum.tile([P, 2, 4, P], BF16, tag="aux", name="bt_ps")
+            for gg in range(2):
+                for t in range(4):
+                    nc.tensor.transpose(bt_ps[:, gg, t, :], bs_sb[b][:, 2 * gp + gg, t * P:(t + 1) * P], ident_b[:])
+            nc.scalar.copy(
+                out=b_grp[b][:, 1024 * gp:1024 * (gp + 1)].rearrange("p (g n t) -> p g n t", g=2, t=4),
+                in_=bt_ps[:].rearrange("p g t n -> p g n t"),
+            )
+
+        def quantise_bases(b):
+            nc.vector.quantize_mx(out=b_code[b][:].bitcast(FP8X4), scales=b_scale[b][:], in_=b_grp[b][:])
+
+        y_t = {}
+
+        def unit_front(b, kc):
+            xh = psum.tile([P, CI], F32, tag="xh", bufs=2, name="xh")
+            for g in range(NG):
+                nc.tensor.matmul(
+                    out=xh[:], lhsT=wb_sb[b][:, g, kc * P:(kc + 1) * P], rhs=x_t[b][:, g, :],
+                    start=(g == 0), stop=(g == NG - 1),
+                )
+            rep = work.tile([P, CI * 8], F32, tag="rep", name="rep")
+            z = work.tile([P, NC * P * 4], BF16, tag="z", name="z", align_bytes=64)
+            zc = work.tile([P, NC * P], U32, tag="zc", name="zc", align_bytes=64)
+            zs = work.tile([P, NC * P], U8, tag="zs", name="zs", align_bytes=64)
+            for h in range(2):
+                nc.scalar.copy(
+                    out=rep[:, 512 * h:512 * (h + 1)].rearrange("k (i r) -> k i r", r=8),
+                    in_=xh[:, 64 * h:64 * (h + 1)].unsqueeze(2).to_broadcast([P, 64, 8]),
+                )
+            for h in range(2):
+                xr = psum.tile([P, 4, P], F32, tag="xr", bufs=3, name="xr")
+                for cc in range(4):
+                    c = 4 * h + cc
+                    nc.tensor.transpose(xr[:, cc, :], rep[:, c * P:(c + 1) * P], ident_f[:])
+                nc.vector.tensor_tensor(
+                    out=z[:, 2048 * h:2048 * (h + 1)].rearrange("p (c k t) -> p c k t", c=4, t=4),
+                    in0=xr[:].unsqueeze(3).to_broadcast([P, 4, P, 4]),
+                    in1=d_rep[:, kc * P:(kc + 1) * P, :].unsqueeze(1).to_broadcast([P, 4, P, 4]),
+                    op=MULT,
+                )
+            for h in range(2):
+                nc.vector.quantize_mx(
+                    out=zc[:, 512 * h:512 * (h + 1)].bitcast(FP8X4),
+                    scales=zs[:, 512 * h:512 * (h + 1)],
+                    in_=z[:, 2048 * h:2048 * (h + 1)],
+                )
+            return zc, zs
+
+        def unit_back(b, kc, zc, zs):
+            if kc == 0:
+                y_t[b] = psum.tile([P, NKC, CO], F32, tag="yt", bufs=1, name="y_t")
+            for c in range(NC):
+                nc.tensor.matmul_mx(
+                    out=y_t[b][:, kc, :],
+                    lhsT=zc[:, c * P:(c + 1) * P].bitcast(FP8X4), lhsT_scale=zs[:, c * P:(c + 1) * P],
+                    rhs=w_code[:, c * CO:(c + 1) * CO].bitcast(FP8X4), rhs_scale=w_scale[:, c * CO:(c + 1) * CO],
+                    start=(c == 0), stop=(c == NC - 1),
+                )
+
+        def finish(b):
+            yg = work.tile([P, CO * 4], BF16, tag="yg", name="yg", align_bytes=64)
+            yc = work.tile([P, CO], U32, tag="yc", name="yc", align_bytes=64)
+            ys = work.tile([P, CO], U8, tag="ys", name="ys", align_bytes=64)
+            nc.scalar.copy(out=yg[:].rearrange("p (o t) -> p o t", t=4), in_=y_t[b][:].rearrange("p t o -> p o t"))
+            nc.vector.quantize_mx(out=yc[:].bitcast(FP8X4), scales=ys[:], in_=yg[:])
+            for nh in range(2):
+                yp = psum.tile([P, 512], F32, tag="aux", name="yp")
+                nc.tensor.matmul_mx(
+                    out=yp[:], lhsT=yc[:].bitcast(FP8X4), lhsT_scale=ys[:],
+                    rhs=b_code[b][:, 512 * nh:512 * (nh + 1)].bitcast(FP8X4),
+                    rhs_scale=b_scale[b][:, 512 * nh:512 * (nh + 1)],
+                    start=True, stop=True,
+                )
+                yo = work.tile([P, 512], F32, tag="yo", bufs=4, name="yo")
+                if b == NB - 1 and nh == 0:
+                    nc.vector.tensor_copy(out=yo[:], in_=yp[:])
+                else:
+                    nc.scalar.copy(out=yo[:], in_=yp[:])
+                nc.sync.dma_start(out=out[b][:, 512 * nh:512 * (nh + 1)], in_=yo[:])
+
+        transpose_x(0, "v")
+        units = [(b, kc) for b in range(NB) for kc in range(NKC)]
+        for n, (b, kc) in enumerate(units):
+            zc, zs = unit_front(b, kc)
+            if n == 0:
+                prepare_weights()
+            unit_back(b, kc, zc, zs)
+            if n == 1:
+                transpose_x(1, "s")
+                transpose_bases(0, 0)
+                transpose_bases(0, 1)
+            if n == 2:
+                transpose_bases(0, 2)
+                transpose_bases(0, 3)
+                quantise_bases(0)
+            if n == 3:
+                finish(0)
+            if n == 4:
+                transpose_bases(1, 0)
+                transpose_bases(1, 1)
+            if n == 5:
+                transpose_bases(1, 2)
+                transpose_bases(1, 3)
+                quantise_bases(1)
+            if n == 7:
+                finish(1)

@@ -15,6 +15,9 @@ P = 128
 NG = NPTS // P
 NKC = NM // P
 NC = CI * KM // 512
+NU = NB * NKC
+AV = 92
+AG = P - AV
 FLOPS = 2 * NB * (CI * NPTS * NM + CI * KM * CO * NM + CO * NM * NPTS)
 
 
@@ -22,8 +25,9 @@ def tile_phydgalerkinconv_kernel(tc, x, wbases, bases, weights, D, out):
     nc = tc.nc
     with ExitStack() as ctx:
         keep = ctx.enter_context(tc.tile_pool(name="keep", bufs=1))
-        work = ctx.enter_context(tc.tile_pool(name="work", bufs=3))
+        work = ctx.enter_context(tc.tile_pool(name="work", bufs=2))
         psum = ctx.enter_context(tc.psum_pool(name="psum", bufs=2))
+        ctx.enter_context(tc.manual_schedule())
 
         ident_b = keep.tile([P, P], BF16, name="ident_b")
         make_identity(nc, ident_b[:])
@@ -32,59 +36,73 @@ def tile_phydgalerkinconv_kernel(tc, x, wbases, bases, weights, D, out):
 
         x_sb = [keep.tile([P, NPTS], BF16, name="x_sb%d" % b) for b in range(NB)]
         wb_sb = [keep.tile([P, NG, NM], BF16, name="wb_sb%d" % b) for b in range(NB)]
-        bs_sb = [keep.tile([P, NG, NM], BF16, name="bs_sb%d" % b) for b in range(NB)]
+        bs_sb = [keep.tile([P, NG * NM], BF16, name="bs_sb%d" % b) for b in range(NB)]
         d_load = keep.tile([P, 4 * NM], BF16, name="d_load")
         w_om = keep.tile([P, CI * KM], BF16, name="w_om")
 
-        nc.sync.dma_start(out=x_sb[0][:], in_=x[0])
-        wb0 = wbases[0].rearrange("(g p) k -> p g k", p=P)
-        for kc in range(NKC):
-            nc.sync.dma_start(out=wb_sb[0][:, :, kc * P:(kc + 1) * P], in_=wb0[:, :, kc * P:(kc + 1) * P])
-        for r in range(8):
-            nc.scalar.dma_start(
+        def load_d(r):
+            nc.sync.dma_start(
                 out=d_load[r:P:8, :],
                 in_=D[4 * r:4 * r + 4, :].rearrange("t k -> (t k)").partition_broadcast(16),
             )
+
+        wb0 = wbases[0].rearrange("(g p) k -> p g k", p=P)
+        load_d(0)
+        load_d(1)
+        nc.sync.dma_start(out=x_sb[0][:], in_=x[0])
+        nc.sync.dma_start(out=wb_sb[0][:, :, 0:256], in_=wb0[:, :, 0:256])
+        for r in range(2, 8):
+            load_d(r)
+        nc.sync.dma_start(out=wb_sb[0][:, :, 256:512], in_=wb0[:, :, 256:512])
+        nc.sync.dma_start(out=x_sb[1][:], in_=x[1])
+        nc.sync.dma_start(out=wb_sb[1][:], in_=wbases[1].rearrange("(g p) k -> p g k", p=P))
         for q in range(4):
             nc.sync.dma_start(
                 out=w_om[:, 1024 * q:1024 * (q + 1)].rearrange("o (i j) -> o i j", j=KM),
                 in_=weights[32 * q:32 * (q + 1)].rearrange("i o j -> o i j"),
             )
-        nc.sync.dma_start(out=x_sb[1][:], in_=x[1])
-        nc.sync.dma_start(out=wb_sb[1][:], in_=wbases[1].rearrange("(g p) k -> p g k", p=P))
         for b in range(NB):
-            nc.sync.dma_start(out=bs_sb[b][:], in_=bases[b].rearrange("(g p) k -> p g k", p=P))
-
-        d_rep = keep.tile([P, NM, 4], BF16, name="d_rep")
-        nc.vector.tensor_copy(out=d_rep[:], in_=d_load[:].rearrange("p (t k) -> p k t", t=4))
+            nc.sync.dma_start(
+                out=bs_sb[b][:].rearrange("p (g k) -> p g k", g=NG),
+                in_=bases[b].rearrange("(g p) k -> p g k", p=P),
+            )
 
         x_t = [keep.tile([P, NG, CI], BF16, name="x_t%d" % b) for b in range(NB)]
 
-        def transpose_x(b, engine):
-            xt_ps = psum.tile([P, NG, CI], BF16, tag="aux", name="xt_ps")
-            for g in range(NG):
-                nc.tensor.transpose(xt_ps[:, g, :], x_sb[b][:, g * P:(g + 1) * P], ident_b[:])
-            if engine == "v":
-                nc.vector.tensor_copy(out=x_t[b][:], in_=xt_ps[:])
+        def transpose_x(b, half, on_vector):
+            xt_ps = psum.tile([P, 4, CI], BF16, tag="aux", name="xt_ps")
+            for gg in range(4):
+                g = 4 * half + gg
+                nc.tensor.transpose(xt_ps[:, gg, :], x_sb[b][:, g * P:(g + 1) * P], ident_b[:])
+            if on_vector:
+                nc.vector.tensor_copy(out=x_t[b][:, 4 * half:4 * half + 4, :], in_=xt_ps[:])
             else:
-                nc.scalar.copy(out=x_t[b][:], in_=xt_ps[:])
+                nc.scalar.copy(out=x_t[b][:, 4 * half:4 * half + 4, :], in_=xt_ps[:])
+
+        d_rep = keep.tile([P, NKC, P, 4], BF16, name="d_rep")
+
+        def regroup_d():
+            view = d_load[:].rearrange("p (t u q e) -> p u e q t", t=4, u=2, e=2)
+            for u in range(2):
+                nc.vector.tensor_copy(out=d_rep[:, 2 * u:2 * u + 2, :, :], in_=view[:, u])
 
         w_grp = keep.tile([P, NC * CO * 4], BF16, name="w_grp", align_bytes=64)
         w_code = keep.tile([P, NC * CO], U32, name="w_code", align_bytes=64)
         w_scale = keep.tile([P, NC * CO], U8, name="w_scale", align_bytes=64)
 
-        def prepare_weights():
+        def transpose_weights(cp):
             words = w_om[:].bitcast(F32).rearrange("o (c p u) -> o c p u", c=NC, u=2)
             grp_words = w_grp[:].bitcast(F32).rearrange("p (c o u) -> p c o u", c=NC, u=2)
-            for cp in range(NC // 2):
-                wt_ps = psum.tile([P, 2, 2, CO], F32, tag="aux", name="wt_ps")
-                for cc in range(2):
-                    for u in range(2):
-                        nc.tensor.transpose(wt_ps[:, cc, u, :], words[:, 2 * cp + cc, :, u], ident_f[:])
-                nc.scalar.copy(
-                    out=grp_words[:, 2 * cp:2 * cp + 2, :, :],
-                    in_=wt_ps[:].rearrange("p c u o -> p c o u"),
-                )
+            wt_ps = psum.tile([P, 2, 2, CO], F32, tag="aux", name="wt_ps")
+            for cc in range(2):
+                for u in range(2):
+                    nc.tensor.transpose(wt_ps[:, cc, u, :], words[:, 2 * cp + cc, :, u], ident_f[:])
+            nc.scalar.copy(
+                out=grp_words[:, 2 * cp:2 * cp + 2, :, :],
+                in_=wt_ps[:].rearrange("p c u o -> p c o u"),
+            )
+
+        def quantise_weights():
             nc.vector.quantize_mx(out=w_code[:].bitcast(FP8X4), scales=w_scale[:], in_=w_grp[:])
 
         b_grp = [keep.tile([P, NPTS * 4], BF16, name="b_grp%d" % b, align_bytes=64) for b in range(NB)]
@@ -92,76 +110,111 @@ def tile_phydgalerkinconv_kernel(tc, x, wbases, bases, weights, D, out):
         b_scale = [keep.tile([P, NPTS], U8, name="b_scale%d" % b, align_bytes=64) for b in range(NB)]
 
         def transpose_bases(b, gp):
-            bt_ps = psum.tile([P, 2, 4, P], BF16, tag="aux", name="bt_ps")
+            words = bs_sb[b][:].bitcast(F32).rearrange("p (g u w) -> p g u w", g=NG, u=2)
+            grp_words = b_grp[b][:].bitcast(F32).rearrange("p (g n u) -> p g n u", g=NG, u=2)
+            bt_ps = psum.tile([P, 2, 2, P], F32, tag="aux", name="bt_ps")
             for gg in range(2):
-                for t in range(4):
-                    nc.tensor.transpose(bt_ps[:, gg, t, :], bs_sb[b][:, 2 * gp + gg, t * P:(t + 1) * P], ident_b[:])
+                for u in range(2):
+                    nc.tensor.transpose(bt_ps[:, gg, u, :], words[:, 2 * gp + gg, u, :], ident_f[:])
             nc.scalar.copy(
-                out=b_grp[b][:, 1024 * gp:1024 * (gp + 1)].rearrange("p (g n t) -> p g n t", g=2, t=4),
-                in_=bt_ps[:].rearrange("p g t n -> p g n t"),
+                out=grp_words[:, 2 * gp:2 * gp + 2, :, :],
+                in_=bt_ps[:].rearrange("p g u n -> p g n u"),
             )
 
         def quantise_bases(b):
             nc.vector.quantize_mx(out=b_code[b][:].bitcast(FP8X4), scales=b_scale[b][:], in_=b_grp[b][:])
 
+        z_code = [keep.tile([P, NC * P], U32, name="z_code%d" % n, align_bytes=64) for n in range(NU)]
+        z_scale = [keep.tile([P, NC * P], U8, name="z_scale%d" % n, align_bytes=64) for n in range(NU)]
+        rep = {}
+        xr = {}
+        xg = {}
+        z = {}
         y_t = {}
 
-        def unit_front(b, kc):
-            xh = psum.tile([P, CI], F32, tag="xh", bufs=2, name="xh")
+        def project(n):
+            b, kc = divmod(n, NKC)
+            u, e = divmod(kc, 2)
+            wbv = wb_sb[b][:].rearrange("p g (u q e) -> p g u e q", u=2, e=2)
+            xh = psum.tile([P, CI], F32, tag="xh", bufs=1, name="xh")
             for g in range(NG):
                 nc.tensor.matmul(
-                    out=xh[:], lhsT=wb_sb[b][:, g, kc * P:(kc + 1) * P], rhs=x_t[b][:, g, :],
+                    out=xh[:], lhsT=wbv[:, g, u, e, :], rhs=x_t[b][:, g, :],
                     start=(g == 0), stop=(g == NG - 1),
                 )
-            rep = work.tile([P, CI * 8], F32, tag="rep", name="rep")
-            z = work.tile([P, NC * P * 4], BF16, tag="z", name="z", align_bytes=64)
-            zc = work.tile([P, NC * P], U32, tag="zc", name="zc", align_bytes=64)
-            zs = work.tile([P, NC * P], U8, tag="zs", name="zs", align_bytes=64)
+            rep[n] = work.tile([P, CI * 8], F32, tag="rep", name="rep")
             for h in range(2):
                 nc.scalar.copy(
-                    out=rep[:, 512 * h:512 * (h + 1)].rearrange("k (i r) -> k i r", r=8),
+                    out=rep[n][:, 512 * h:512 * (h + 1)].rearrange("k (i r) -> k i r", r=8),
                     in_=xh[:, 64 * h:64 * (h + 1)].unsqueeze(2).to_broadcast([P, 64, 8]),
                 )
+
+        def spread(n, h):
+            xr[n, h] = psum.tile([P, 4, P], F32, tag="xr", bufs=4, name="xr")
+            for cc in range(4):
+                c = 4 * h + cc
+                nc.tensor.transpose(xr[n, h][:, cc, :], rep[n][:, c * P:(c + 1) * P], ident_f[:])
+            if h == 0:
+                xg[n] = work.tile([P, NC, AG], F32, tag="xg", bufs=3, name="xg")
+            nc.scalar.copy(out=xg[n][:, 4 * h:4 * h + 4, :], in_=xr[n, h][:, :, AV:P])
+
+        def multiply(n):
+            kc = n % NKC
+            z[n] = work.tile([P, NC * P * 4], BF16, tag="z", name="z", align_bytes=64)
+            zv = z[n][:].rearrange("p (c k t) -> p c k t", c=NC, t=4)
+            nc.gpsimd.tensor_tensor(
+                out=zv[:, :, AV:P, :],
+                in0=xg[n][:].unsqueeze(3).to_broadcast([P, NC, AG, 4]),
+                in1=d_rep[:, kc, AV:P, :].unsqueeze(1).to_broadcast([P, NC, AG, 4]),
+                op=MULT,
+            )
             for h in range(2):
-                xr = psum.tile([P, 4, P], F32, tag="xr", bufs=3, name="xr")
-                for cc in range(4):
-                    c = 4 * h + cc
-                    nc.tensor.transpose(xr[:, cc, :], rep[:, c * P:(c + 1) * P], ident_f[:])
                 nc.vector.tensor_tensor(
-                    out=z[:, 2048 * h:2048 * (h + 1)].rearrange("p (c k t) -> p c k t", c=4, t=4),
-                    in0=xr[:].unsqueeze(3).to_broadcast([P, 4, P, 4]),
-                    in1=d_rep[:, kc * P:(kc + 1) * P, :].unsqueeze(1).to_broadcast([P, 4, P, 4]),
+                    out=zv[:, 4 * h:4 * h + 4, 0:AV, :],
+                    in0=xr[n, h][:, :, 0:AV].unsqueeze(3).to_broadcast([P, 4, AV, 4]),
+                    in1=d_rep[:, kc, 0:AV, :].unsqueeze(1).to_broadcast([P, 4, AV, 4]),
                     op=MULT,
                 )
-            for h in range(2):
-                nc.vector.quantize_mx(
-                    out=zc[:, 512 * h:512 * (h + 1)].bitcast(FP8X4),
-                    scales=zs[:, 512 * h:512 * (h + 1)],
-                    in_=z[:, 2048 * h:2048 * (h + 1)],
-                )
-            return zc, zs
 
-        def unit_back(b, kc, zc, zs):
+        def quantise(n, pieces):
+            wide = NC * P // pieces
+            for s in range(pieces):
+                nc.vector.quantize_mx(
+                    out=z_code[n][:, wide * s:wide * (s + 1)].bitcast(FP8X4),
+                    scales=z_scale[n][:, wide * s:wide * (s + 1)],
+                    in_=z[n][:, 4 * wide * s:4 * wide * (s + 1)],
+                )
+
+        def contract(n):
+            b, kc = divmod(n, NKC)
             if kc == 0:
                 y_t[b] = psum.tile([P, NKC, CO], F32, tag="yt", bufs=1, name="y_t")
             for c in range(NC):
                 nc.tensor.matmul_mx(
                     out=y_t[b][:, kc, :],
-                    lhsT=zc[:, c * P:(c + 1) * P].bitcast(FP8X4), lhsT_scale=zs[:, c * P:(c + 1) * P],
+                    lhsT=z_code[n][:, c * P:(c + 1) * P].bitcast(FP8X4), lhsT_scale=z_scale[n][:, c * P:(c + 1) * P],
                     rhs=w_code[:, c * CO:(c + 1) * CO].bitcast(FP8X4), rhs_scale=w_scale[:, c * CO:(c + 1) * CO],
                     start=(c == 0), stop=(c == NC - 1),
                 )
 
-        def finish(b):
-            yg = work.tile([P, CO * 4], BF16, tag="yg", name="yg", align_bytes=64)
-            yc = work.tile([P, CO], U32, tag="yc", name="yc", align_bytes=64)
-            ys = work.tile([P, CO], U8, tag="ys", name="ys", align_bytes=64)
-            nc.scalar.copy(out=yg[:].rearrange("p (o t) -> p o t", t=4), in_=y_t[b][:].rearrange("p t o -> p o t"))
-            nc.vector.quantize_mx(out=yc[:].bitcast(FP8X4), scales=ys[:], in_=yg[:])
+        yg = {}
+        yc = {}
+        ys = {}
+
+        def round_y(b):
+            yg[b] = work.tile([P, CO * 4], BF16, tag="yg", name="yg", align_bytes=64)
+            nc.scalar.copy(out=yg[b][:].rearrange("p (o t) -> p o t", t=4), in_=y_t[b][:].rearrange("p t o -> p o t"))
+
+        def quantise_y(b):
+            yc[b] = work.tile([P, CO], U32, tag="yc", name="yc", align_bytes=64)
+            ys[b] = work.tile([P, CO], U8, tag="ys", name="ys", align_bytes=64)
+            nc.vector.quantize_mx(out=yc[b][:].bitcast(FP8X4), scales=ys[b][:], in_=yg[b][:])
+
+        def reconstruct(b):
             for nh in range(2):
                 yp = psum.tile([P, 512], F32, tag="aux", name="yp")
                 nc.tensor.matmul_mx(
-                    out=yp[:], lhsT=yc[:].bitcast(FP8X4), lhsT_scale=ys[:],
+                    out=yp[:], lhsT=yc[b][:].bitcast(FP8X4), lhsT_scale=ys[b][:],
                     rhs=b_code[b][:, 512 * nh:512 * (nh + 1)].bitcast(FP8X4),
                     rhs_scale=b_scale[b][:, 512 * nh:512 * (nh + 1)],
                     start=True, stop=True,
@@ -173,29 +226,55 @@ def tile_phydgalerkinconv_kernel(tc, x, wbases, bases, weights, D, out):
                     nc.scalar.copy(out=yo[:], in_=yp[:])
                 nc.sync.dma_start(out=out[b][:, 512 * nh:512 * (nh + 1)], in_=yo[:])
 
-        transpose_x(0, "v")
-        units = [(b, kc) for b in range(NB) for kc in range(NKC)]
-        for n, (b, kc) in enumerate(units):
-            zc, zs = unit_front(b, kc)
-            if n == 0:
-                prepare_weights()
-            unit_back(b, kc, zc, zs)
-            if n == 1:
-                transpose_x(1, "s")
+        transpose_x(0, 0, True)
+        transpose_x(0, 1, False)
+        regroup_d()
+        project(0)
+        for r in range(NU):
+            spread(r, 0)
+            if r < 2:
+                spread(r, 1)
+            if r + 1 < NU:
+                project(r + 1)
+            if r >= 2:
+                spread(r, 1)
+            if r == 1:
+                transpose_x(1, 0, False)
+                transpose_x(1, 1, False)
+            if r == 4:
+                transpose_weights(0)
+                transpose_weights(1)
+                transpose_weights(2)
+            if r == 5:
+                transpose_weights(3)
                 transpose_bases(0, 0)
                 transpose_bases(0, 1)
-            if n == 2:
+            if r == 6:
                 transpose_bases(0, 2)
                 transpose_bases(0, 3)
-                quantise_bases(0)
-            if n == 3:
-                finish(0)
-            if n == 4:
-                transpose_bases(1, 0)
-                transpose_bases(1, 1)
-            if n == 5:
-                transpose_bases(1, 2)
-                transpose_bases(1, 3)
+                for gp in range(4):
+                    transpose_bases(1, gp)
+            if r == 7:
+                for n in range(4):
+                    contract(n)
+                round_y(0)
+                contract(4)
+                contract(5)
+            multiply(r)
+            if r == 7:
                 quantise_bases(1)
-            if n == 7:
-                finish(1)
+                quantise_y(0)
+            if r >= 1:
+                quantise(r - 1, 1)
+            if r == 5:
+                quantise_weights()
+            if r == 6:
+                quantise_bases(0)
+            if r == 7:
+                reconstruct(0)
+        quantise(7, 2)
+        contract(6)
+        contract(7)
+        round_y(1)
+        quantise_y(1)
+        reconstruct(1)

@@ -56,25 +56,28 @@ def tile_phydgalerkinconv_kernel(tc, x, wbases, bases, weights, D, out):
         nc.sync.dma_start(out=wb_sb[0][:, :, 256:512], in_=wb0[:, :, 256:512])
         nc.sync.dma_start(out=x_sb[1][:], in_=x[1])
         nc.sync.dma_start(out=wb_sb[1][:], in_=wbases[1].rearrange("(g p) k -> p g k", p=P))
-        for q in range(4):
-            nc.sync.dma_start(
-                out=w_om[:, 1024 * q:1024 * (q + 1)].rearrange("o (i j) -> o i j", j=KM),
-                in_=weights[32 * q:32 * (q + 1)].rearrange("i o j -> o i j"),
-            )
-        for b in range(NB):
+        def load_bases(b):
             nc.sync.dma_start(
                 out=bs_sb[b][:].rearrange("p (g k) -> p g k", g=NG),
                 in_=bases[b].rearrange("(g p) k -> p g k", p=P),
             )
 
+        load_bases(0)
+        for q in range(4):
+            nc.sync.dma_start(
+                out=w_om[:, 1024 * q:1024 * (q + 1)].rearrange("o (i j) -> o i j", j=KM),
+                in_=weights[32 * q:32 * (q + 1)].rearrange("i o j -> o i j"),
+            )
+        load_bases(1)
+
         x_t = [keep.tile([P, NG, CI], BF16, name="x_t%d" % b) for b in range(NB)]
 
-        def transpose_x(b, half, on_vector):
+        def transpose_x(b, half):
             xt_ps = psum.tile([P, 4, CI], BF16, tag="aux", name="xt_ps")
             for gg in range(4):
                 g = 4 * half + gg
                 nc.tensor.transpose(xt_ps[:, gg, :], x_sb[b][:, g * P:(g + 1) * P], ident_b[:])
-            if on_vector:
+            if b == 0 and half == 0:
                 nc.vector.tensor_copy(out=x_t[b][:, 4 * half:4 * half + 4, :], in_=xt_ps[:])
             else:
                 nc.scalar.copy(out=x_t[b][:, 4 * half:4 * half + 4, :], in_=xt_ps[:])
@@ -226,8 +229,13 @@ def tile_phydgalerkinconv_kernel(tc, x, wbases, bases, weights, D, out):
                     nc.scalar.copy(out=yo[:], in_=yp[:])
                 nc.sync.dma_start(out=out[b][:, 512 * nh:512 * (nh + 1)], in_=yo[:])
 
-        transpose_x(0, 0, True)
-        transpose_x(0, 1, False)
+        side_jobs = [(transpose_x, (1, 0)), (transpose_x, (1, 1))]
+        side_jobs.extend([(transpose_bases, (0, gp)) for gp in range(4)])
+        side_jobs.extend([(transpose_weights, (cp,)) for cp in range(4)])
+        side_jobs.extend([(transpose_bases, (1, gp)) for gp in range(4)])
+
+        transpose_x(0, 0)
+        transpose_x(0, 1)
         regroup_d()
         project(0)
         for r in range(NU):
@@ -238,43 +246,26 @@ def tile_phydgalerkinconv_kernel(tc, x, wbases, bases, weights, D, out):
                 project(r + 1)
             if r >= 2:
                 spread(r, 1)
-            if r == 1:
-                transpose_x(1, 0, False)
-                transpose_x(1, 1, False)
-            if r == 4:
-                transpose_weights(0)
-                transpose_weights(1)
-                transpose_weights(2)
-            if r == 5:
-                transpose_weights(3)
-                transpose_bases(0, 0)
-                transpose_bases(0, 1)
-            if r == 6:
-                transpose_bases(0, 2)
-                transpose_bases(0, 3)
-                for gp in range(4):
-                    transpose_bases(1, gp)
-            if r == 7:
-                for n in range(4):
-                    contract(n)
-                round_y(0)
-                contract(4)
-                contract(5)
+            if r >= 1:
+                for job, arguments in side_jobs[2 * r - 2:2 * r]:
+                    job(*arguments)
             multiply(r)
-            if r == 7:
-                quantise_bases(1)
-                quantise_y(0)
             if r >= 1:
                 quantise(r - 1, 1)
+            if r == 3:
+                quantise_bases(0)
             if r == 5:
                 quantise_weights()
-            if r == 6:
-                quantise_bases(0)
-            if r == 7:
-                reconstruct(0)
-        quantise(7, 2)
-        contract(6)
-        contract(7)
+        for n in range(NKC):
+            contract(n)
+        round_y(0)
+        quantise_y(0)
+        for n in range(NKC, NU - 1):
+            contract(n)
+        reconstruct(0)
+        quantise(NU - 1, 2)
+        contract(NU - 1)
         round_y(1)
+        quantise_bases(1)
         quantise_y(1)
         reconstruct(1)

@@ -34,6 +34,12 @@ def tile_phydgalerkinconv_kernel(tc, x, wbases, bases, weights, D, out):
         ident_f = keep.tile([P, P], F32, name="ident_f")
         make_identity(nc, ident_f[:])
 
+        warm_in = keep.tile([P, 512], BF16, name="warm_in")
+        nc.vector.memset(warm_in[:], 0.0)
+        warm_ps = psum.tile([P, 512], F32, tag="xr", bufs=4, name="warm_ps")
+        for w in range(4):
+            nc.tensor.matmul(out=warm_ps[:], lhsT=warm_in[:, 0:P], rhs=warm_in[:], start=True, stop=True)
+
         x_sb = [keep.tile([P, NPTS], BF16, name="x_sb%d" % b) for b in range(NB)]
         wb_sb = [keep.tile([P, NG, NM], BF16, name="wb_sb%d" % b) for b in range(NB)]
         bs_sb = [keep.tile([P, NG * NM], BF16, name="bs_sb%d" % b) for b in range(NB)]
@@ -84,10 +90,12 @@ def tile_phydgalerkinconv_kernel(tc, x, wbases, bases, weights, D, out):
 
         d_rep = keep.tile([P, NKC, P, 4], BF16, name="d_rep")
 
-        def regroup_d():
+        def regroup_d(u):
             view = d_load[:].rearrange("p (t u q e) -> p u e q t", t=4, u=2, e=2)
-            for u in range(2):
-                nc.vector.tensor_copy(out=d_rep[:, 2 * u:2 * u + 2, :, :], in_=view[:, u])
+            if u == 0:
+                nc.vector.tensor_copy(out=d_rep[:, 0:2, :, :], in_=view[:, 0])
+            else:
+                nc.scalar.copy(out=d_rep[:, 2:4, :, :], in_=view[:, 1])
 
         w_grp = keep.tile([P, NC * CO * 4], BF16, name="w_grp", align_bytes=64)
         w_code = keep.tile([P, NC * CO], U32, name="w_code", align_bytes=64)
@@ -236,7 +244,7 @@ def tile_phydgalerkinconv_kernel(tc, x, wbases, bases, weights, D, out):
 
         transpose_x(0, 0)
         transpose_x(0, 1)
-        regroup_d()
+        regroup_d(0)
         project(0)
         for r in range(NU):
             spread(r, 0)
@@ -246,24 +254,29 @@ def tile_phydgalerkinconv_kernel(tc, x, wbases, bases, weights, D, out):
                 project(r + 1)
             if r >= 2:
                 spread(r, 1)
+            if r == 0:
+                regroup_d(1)
             if r >= 1:
                 for job, arguments in side_jobs[2 * r - 2:2 * r]:
                     job(*arguments)
+            if r == NU - 1:
+                for n in range(NKC):
+                    contract(n)
+                round_y(0)
+                for n in range(NKC, NU - 2):
+                    contract(n)
             multiply(r)
+            if r == NU - 1:
+                quantise_y(0)
+                reconstruct(0)
             if r >= 1:
                 quantise(r - 1, 1)
             if r == 3:
                 quantise_bases(0)
             if r == 5:
                 quantise_weights()
-        for n in range(NKC):
-            contract(n)
-        round_y(0)
-        quantise_y(0)
-        for n in range(NKC, NU - 1):
-            contract(n)
-        reconstruct(0)
         quantise(NU - 1, 2)
+        contract(NU - 2)
         contract(NU - 1)
         round_y(1)
         quantise_bases(1)

@@ -137,6 +137,7 @@ def tile_phydgalerkinconv_kernel(tc, x, wbases, bases, weights, D, out):
 
         z_code = [keep.tile([P, NC * P], U32, name="z_code%d" % n, align_bytes=64) for n in range(NU)]
         z_scale = [keep.tile([P, NC * P], U8, name="z_scale%d" % n, align_bytes=64) for n in range(NU)]
+        xh = {}
         rep = {}
         xr = {}
         xg = {}
@@ -147,17 +148,19 @@ def tile_phydgalerkinconv_kernel(tc, x, wbases, bases, weights, D, out):
             b, kc = divmod(n, NKC)
             u, e = divmod(kc, 2)
             wbv = wb_sb[b][:].rearrange("p g (u q e) -> p g u e q", u=2, e=2)
-            xh = psum.tile([P, CI], F32, tag="xh", bufs=1, name="xh")
+            xh[n] = psum.tile([P, CI], F32, tag="acc", name="xh")
             for g in range(NG):
                 nc.tensor.matmul(
-                    out=xh[:], lhsT=wbv[:, g, u, e, :], rhs=x_t[b][:, g, :],
+                    out=xh[n][:], lhsT=wbv[:, g, u, e, :], rhs=x_t[b][:, g, :],
                     start=(g == 0), stop=(g == NG - 1),
                 )
-            rep[n] = work.tile([P, CI * 8], F32, tag="rep", name="rep")
+
+        def replicate(n):
+            rep[n] = work.tile([P, CI * 8], F32, tag="rep", bufs=3, name="rep")
             for h in range(2):
                 nc.scalar.copy(
                     out=rep[n][:, 512 * h:512 * (h + 1)].rearrange("k (i r) -> k i r", r=8),
-                    in_=xh[:, 64 * h:64 * (h + 1)].unsqueeze(2).to_broadcast([P, 64, 8]),
+                    in_=xh[n][:, 64 * h:64 * (h + 1)].unsqueeze(2).to_broadcast([P, 64, 8]),
                 )
 
         def spread(n, h):
@@ -199,7 +202,7 @@ def tile_phydgalerkinconv_kernel(tc, x, wbases, bases, weights, D, out):
         def contract(n):
             b, kc = divmod(n, NKC)
             if kc == 0:
-                y_t[b] = psum.tile([P, NKC, CO], F32, tag="yt", bufs=1, name="y_t")
+                y_t[b] = psum.tile([P, NKC, CO], F32, tag="acc", name="y_t")
             for c in range(NC):
                 nc.tensor.matmul_mx(
                     out=y_t[b][:, kc, :],
@@ -246,14 +249,18 @@ def tile_phydgalerkinconv_kernel(tc, x, wbases, bases, weights, D, out):
         transpose_x(0, 1)
         regroup_d(0)
         project(0)
+        replicate(0)
+        project(1)
         for r in range(NU):
             spread(r, 0)
             if r < 2:
                 spread(r, 1)
-            if r + 1 < NU:
-                project(r + 1)
+            if r + 2 < NU:
+                project(r + 2)
             if r >= 2:
                 spread(r, 1)
+            if r + 1 < NU:
+                replicate(r + 1)
             if r == 0:
                 regroup_d(1)
             if r >= 1:

from contextlib import ExitStack

import concourse.mybir as mybir
from concourse.masks import make_identity

F32 = mybir.dt.float32
BF16 = mybir.dt.bfloat16
U32 = mybir.dt.uint32
U8 = mybir.dt.uint8
FP8X4 = mybir.dt.float8_e4m3fn_x4
MULT = mybir.AluOpType.mult

NB, CI, CO, NPTS, KM, NM = 2, 128, 128, 1024, 32, 512
P = 128
NG = NPTS // P
NKC = NM // P
NC = CI * KM // 512
NU = NB * NKC
AV = 92
AG = P - AV
FLOPS = 2 * NB * (CI * NPTS * NM + CI * KM * CO * NM + CO * NM * NPTS)


def tile_phydgalerkinconv_kernel(tc, x, wbases, bases, weights, D, out):
    nc = tc.nc
    with ExitStack() as ctx:
        keep = ctx.enter_context(tc.tile_pool(name="keep", bufs=1))
        work = ctx.enter_context(tc.tile_pool(name="work", bufs=2))
        psum = ctx.enter_context(tc.psum_pool(name="psum", bufs=2))
        ctx.enter_context(tc.manual_schedule())

        ident_b = keep.tile([P, P], BF16, name="ident_b")
        make_identity(nc, ident_b[:])
        ident_f = keep.tile([P, P], F32, name="ident_f")
        make_identity(nc, ident_f[:])

        warm_in = keep.tile([P, 512], BF16, name="warm_in")
        nc.vector.memset(warm_in[:], 0.0)
        warm_ps = psum.tile([P, 512], F32, tag="xr", bufs=4, name="warm_ps")
        for w in range(4):
            nc.tensor.matmul(out=warm_ps[:], lhsT=warm_in[:, 0:P], rhs=warm_in[:], start=True, stop=True)

        x_sb = [keep.tile([P, NPTS], BF16, name="x_sb%d" % b) for b in range(NB)]
        wb_sb = [keep.tile([P, NG, NM], BF16, name="wb_sb%d" % b) for b in range(NB)]
        bs_sb = [keep.tile([P, NG * NM], BF16, name="bs_sb%d" % b) for b in range(NB)]
        d_load = keep.tile([P, 4 * NM], BF16, name="d_load")
        w_om = keep.tile([P, CI * KM], BF16, name="w_om")

        def load_d(r):
            nc.sync.dma_start(
                out=d_load[r:P:8, :],
                in_=D[4 * r:4 * r + 4, :].rearrange("t k -> (t k)").partition_broadcast(16),
            )

        wb0 = wbases[0].rearrange("(g p) k -> p g k", p=P)
        load_d(0)
        load_d(1)
        nc.sync.dma_start(out=x_sb[0][:], in_=x[0])
        nc.sync.dma_start(out=wb_sb[0][:, :, 0:256], in_=wb0[:, :, 0:256])
        for r in range(2, 8):
            load_d(r)
        nc.sync.dma_start(out=wb_sb[0][:, :, 256:512], in_=wb0[:, :, 256:512])
        nc.sync.dma_start(out=x_sb[1][:], in_=x[1])
        nc.sync.dma_start(out=wb_sb[1][:], in_=wbases[1].rearrange("(g p) k -> p g k", p=P))
        def load_bases(b):
            nc.sync.dma_start(
                out=bs_sb[b][:].rearrange("p (g k) -> p g k", g=NG),
                in_=bases[b].rearrange("(g p) k -> p g k", p=P),
            )

        load_bases(0)
        for q in range(4):
            nc.sync.dma_start(
                out=w_om[:, 1024 * q:1024 * (q + 1)].rearrange("o (i j) -> o i j", j=KM),
                in_=weights[32 * q:32 * (q + 1)].rearrange("i o j -> o i j"),
            )
        load_bases(1)

        x_t = [keep.tile([P, NG, CI], BF16, name="x_t%d" % b) for b in range(NB)]

        def transpose_x(b, half):
            xt_ps = psum.tile([P, 4, CI], BF16, tag="aux", name="xt_ps")
            for gg in range(4):
                g = 4 * half + gg
                nc.tensor.transpose(xt_ps[:, gg, :], x_sb[b][:, g * P:(g + 1) * P], ident_b[:])
            if b == 0 and half == 0:
                nc.vector.tensor_copy(out=x_t[b][:, 4 * half:4 * half + 4, :], in_=xt_ps[:])
            else:
                nc.scalar.copy(out=x_t[b][:, 4 * half:4 * half + 4, :], in_=xt_ps[:])

        d_rep = keep.tile([P, NKC, P, 4], BF16, name="d_rep")

        def regroup_d(u):
            view = d_load[:].rearrange("p (t u q e) -> p u e q t", t=4, u=2, e=2)
            if u == 0:
                nc.vector.tensor_copy(out=d_rep[:, 0:2, :, :], in_=view[:, 0])
            else:
                nc.scalar.copy(out=d_rep[:, 2:4, :, :], in_=view[:, 1])

        w_grp = keep.tile([P, NC * CO * 4], BF16, name="w_grp", align_bytes=64)
        w_code = keep.tile([P, NC * CO], U32, name="w_code", align_bytes=64)
        w_scale = keep.tile([P, NC * CO], U8, name="w_scale", align_bytes=64)

        def transpose_weights(cp):
            words = w_om[:].bitcast(F32).rearrange("o (c p u) -> o c p u", c=NC, u=2)
            grp_words = w_grp[:].bitcast(F32).rearrange("p (c o u) -> p c o u", c=NC, u=2)
            wt_ps = psum.tile([P, 2, 2, CO], F32, tag="aux", name="wt_ps")
            for cc in range(2):
                for u in range(2):
                    nc.tensor.transpose(wt_ps[:, cc, u, :], words[:, 2 * cp + cc, :, u], ident_f[:])
            nc.scalar.copy(
                out=grp_words[:, 2 * cp:2 * cp + 2, :, :],
                in_=wt_ps[:].rearrange("p c u o -> p c o u"),
            )

        def quantise_weights():
            nc.vector.quantize_mx(out=w_code[:].bitcast(FP8X4), scales=w_scale[:], in_=w_grp[:])

        b_grp = [keep.tile([P, NPTS * 4], BF16, name="b_grp%d" % b, align_bytes=64) for b in range(NB)]
        b_code = [keep.tile([P, NPTS], U32, name="b_code%d" % b, align_bytes=64) for b in range(NB)]
        b_scale = [keep.tile([P, NPTS], U8, name="b_scale%d" % b, align_bytes=64) for b in range(NB)]

        def transpose_bases(b, gp):
            words = bs_sb[b][:].bitcast(F32).rearrange("p (g u w) -> p g u w", g=NG, u=2)
            grp_words = b_grp[b][:].bitcast(F32).rearrange("p (g n u) -> p g n u", g=NG, u=2)
            bt_ps = psum.tile([P, 2, 2, P], F32, tag="aux", name="bt_ps")
            for gg in range(2):
                for u in range(2):
                    nc.tensor.transpose(bt_ps[:, gg, u, :], words[:, 2 * gp + gg, u, :], ident_f[:])
            nc.scalar.copy(
                out=grp_words[:, 2 * gp:2 * gp + 2, :, :],
                in_=bt_ps[:].rearrange("p g u n -> p g n u"),
            )

        def quantise_bases(b):
            nc.vector.quantize_mx(out=b_code[b][:].bitcast(FP8X4), scales=b_scale[b][:], in_=b_grp[b][:])

        z_code = [keep.tile([P, NC * P], U32, name="z_code%d" % n, align_bytes=64) for n in range(NU)]
        z_scale = [keep.tile([P, NC * P], U8, name="z_scale%d" % n, align_bytes=64) for n in range(NU)]
        xh = {}
        rep = {}
        xr = {}
        xg = {}
        z = {}
        y_t = {}

        def project(n):
            b, kc = divmod(n, NKC)
            u, e = divmod(kc, 2)
            wbv = wb_sb[b][:].rearrange("p g (u q e) -> p g u e q", u=2, e=2)
            xh[n] = psum.tile([P, CI], F32, tag="acc", name="xh")
            for g in range(NG):
                nc.tensor.matmul(
                    out=xh[n][:], lhsT=wbv[:, g, u, e, :], rhs=x_t[b][:, g, :],
                    start=(g == 0), stop=(g == NG - 1),
                )

        def replicate(n):
            rep[n] = work.tile([P, CI * 8], F32, tag="rep", bufs=3, name="rep")
            for h in range(2):
                nc.scalar.copy(
                    out=rep[n][:, 512 * h:512 * (h + 1)].rearrange("k (i r) -> k i r", r=8),
                    in_=xh[n][:, 64 * h:64 * (h + 1)].unsqueeze(2).to_broadcast([P, 64, 8]),
                )

        def spread(n, h):
            xr[n, h] = psum.tile([P, 4, P], F32, tag="xr", bufs=4, name="xr")
            for cc in range(4):
                c = 4 * h + cc
                nc.tensor.transpose(xr[n, h][:, cc, :], rep[n][:, c * P:(c + 1) * P], ident_f[:])
            if h == 0:
                xg[n] = work.tile([P, NC, AG], F32, tag="xg", bufs=3, name="xg")
            nc.scalar.copy(out=xg[n][:, 4 * h:4 * h + 4, :], in_=xr[n, h][:, :, AV:P])

        def multiply(n):
            kc = n % NKC
            z[n] = work.tile([P, NC * P * 4], BF16, tag="z", name="z", align_bytes=64)
            zv = z[n][:].rearrange("p (c k t) -> p c k t", c=NC, t=4)
            nc.gpsimd.tensor_tensor(
                out=zv[:, :, AV:P, :],
                in0=xg[n][:].unsqueeze(3).to_broadcast([P, NC, AG, 4]),
                in1=d_rep[:, kc, AV:P, :].unsqueeze(1).to_broadcast([P, NC, AG, 4]),
                op=MULT,
            )
            for h in range(2):
                nc.vector.tensor_tensor(
                    out=zv[:, 4 * h:4 * h + 4, 0:AV, :],
                    in0=xr[n, h][:, :, 0:AV].unsqueeze(3).to_broadcast([P, 4, AV, 4]),
                    in1=d_rep[:, kc, 0:AV, :].unsqueeze(1).to_broadcast([P, 4, AV, 4]),
                    op=MULT,
                )

        def quantise(n, pieces):
            wide = NC * P // pieces
            for s in range(pieces):
                nc.vector.quantize_mx(
                    out=z_code[n][:, wide * s:wide * (s + 1)].bitcast(FP8X4),
                    scales=z_scale[n][:, wide * s:wide * (s + 1)],
                    in_=z[n][:, 4 * wide * s:4 * wide * (s + 1)],
                )

        def contract(n):
            b, kc = divmod(n, NKC)
            if kc == 0:
                y_t[b] = psum.tile([P, NKC, CO], F32, tag="acc", name="y_t")
            for c in range(NC):
                nc.tensor.matmul_mx(
                    out=y_t[b][:, kc, :],
                    lhsT=z_code[n][:, c * P:(c + 1) * P].bitcast(FP8X4), lhsT_scale=z_scale[n][:, c * P:(c + 1) * P],
                    rhs=w_code[:, c * CO:(c + 1) * CO].bitcast(FP8X4), rhs_scale=w_scale[:, c * CO:(c + 1) * CO],
                    start=(c == 0), stop=(c == NC - 1),
                )

        yg = {}
        yc = {}
        ys = {}

        def round_y(b):
            yg[b] = work.tile([P, CO * 4], BF16, tag="yg", name="yg", align_bytes=64)
            nc.scalar.copy(out=yg[b][:].rearrange("p (o t) -> p o t", t=4), in_=y_t[b][:].rearrange("p t o -> p o t"))

        def quantise_y(b):
            yc[b] = work.tile([P, CO], U32, tag="yc", name="yc", align_bytes=64)
            ys[b] = work.tile([P, CO], U8, tag="ys", name="ys", align_bytes=64)
            nc.vector.quantize_mx(out=yc[b][:].bitcast(FP8X4), scales=ys[b][:], in_=yg[b][:])

        def reconstruct(b):
            for nh in range(2):
                yp = psum.tile([P, 512], F32, tag="aux", name="yp")
                nc.tensor.matmul_mx(
                    out=yp[:], lhsT=yc[b][:].bitcast(FP8X4), lhsT_scale=ys[b][:],
                    rhs=b_code[b][:, 512 * nh:512 * (nh + 1)].bitcast(FP8X4),
                    rhs_scale=b_scale[b][:, 512 * nh:512 * (nh + 1)],
                    start=True, stop=True,
                )
                yo = work.tile([P, 512], F32, tag="yo", bufs=4, name="yo")
                if b == NB - 1 and nh == 0:
                    nc.vector.tensor_copy(out=yo[:], in_=yp[:])
                else:
                    nc.scalar.copy(out=yo[:], in_=yp[:])
                nc.sync.dma_start(out=out[b][:, 512 * nh:512 * (nh + 1)], in_=yo[:])

        side_jobs = [(transpose_x, (1, 0)), (transpose_x, (1, 1))]
        side_jobs.extend([(transpose_bases, (0, gp)) for gp in range(4)])
        side_jobs.extend([(transpose_weights, (cp,)) for cp in range(4)])
        side_jobs.extend([(transpose_bases, (1, gp)) for gp in range(4)])

        transpose_x(0, 0)
        transpose_x(0, 1)
        regroup_d(0)
        project(0)
        replicate(0)
        project(1)
        for r in range(NU):
            spread(r, 0)
            if r < 2:
                spread(r, 1)
            if r + 2 < NU:
                project(r + 2)
            if r >= 2:
                spread(r, 1)
            if r + 1 < NU:
                replicate(r + 1)
            if r == 0:
                regroup_d(1)
            if r >= 1:
                for job, arguments in side_jobs[2 * r - 2:2 * r]:
                    job(*arguments)
            if r == NU - 1:
                for n in range(NKC):
                    contract(n)
                round_y(0)
                for n in range(NKC, NU - 2):
                    contract(n)
            multiply(r)
            if r == NU - 1:
                quantise_y(0)
                reconstruct(0)
            if r >= 1:
                quantise(r - 1, 1)
            if r == 3:
                quantise_bases(0)
            if r == 5:
                quantise_weights()
        quantise(NU - 1, 2)
        contract(NU - 2)
        contract(NU - 1)
        round_y(1)
        quantise_bases(1)
        quantise_y(1)
        reconstruct(1)
